import numpy as np
import ml_dtypes


BF16 = ml_dtypes.bfloat16


def bf(x):
    return np.asarray(x, np.float32).astype(BF16)


def f64(x):
    return np.asarray(x).astype(np.float64)


E2M1 = np.array([0.0, 0.5, 1.0, 1.5, 2.0, 3.0, 4.0, 6.0, -0.0, -0.5, -1.0, -1.5, -2.0, -3.0, -4.0, -6.0])


def pack_weight(w, fmt):
    k, n = w.shape
    w = f64(bf(w)).reshape(k // 32, 32, n)
    amax = np.abs(w).max(1)
    if fmt == "e4m3":
        byte = np.frexp(amax)[1] - 1 + 127 - 7
    else:
        mant, ex = np.frexp(amax / 6.0)
        byte = np.where(mant > 0.5, ex, ex - 1) + 127
    byte = np.clip(np.where(amax > 0, byte, 1), 1, 254)
    scaled = (w * np.exp2(127.0 - byte)[:, None, :]).reshape(k, n).astype(np.float32)
    by_word = np.ascontiguousarray(scaled.reshape(k // 512, 128, 4, n).transpose(0, 1, 3, 2))
    if fmt == "e4m3":
        words = by_word.astype(ml_dtypes.float8_e4m3fn).view(np.uint8)
    else:
        c = by_word.astype(ml_dtypes.float4_e2m1fn).view(np.uint8) & 0xF
        words = c[..., 0::2] | (c[..., 1::2] << 4)
    return np.ascontiguousarray(words), np.ascontiguousarray(byte.astype(np.uint8).reshape(k // 512, 16, n))


def unpack_weight(words, scales, fmt):
    g, p, n, _ = words.shape
    if fmt == "e4m3":
        vals = np.ascontiguousarray(words).view(ml_dtypes.float8_e4m3fn).astype(np.float64)
    else:
        nib = np.empty((g, p, n, 4), np.uint8)
        nib[..., 0::2] = words & 0xF
        nib[..., 1::2] = words >> 4
        vals = E2M1[nib]
    vals = vals * np.repeat(np.exp2(scales.astype(np.float64) - 127.0), 8, axis=1)[..., None]
    return vals.transpose(0, 1, 3, 2).reshape(g * 512, n)

def pack4(w):
    words, scales = pack_weight(w, "e2m1")
    return words.reshape(words.shape[0], 128, -1), scales


def unpack4(words, scales):
    return unpack_weight(words.reshape(words.shape[0], 128, -1, 2), scales, "e2m1")


def kspread(k):
    return np.exp2(np.repeat(np.random.randint(-6, 7, k // 32), 32).astype(np.float64))


T, B, H, DH, R, L = 64, 2, 16, 224, 112, 512
M = H * DH


def rope_tables():
    inv_freq = 1.0 / (10000.0 ** (f64(np.arange(0, R, 2)) / R))
    pos = f64(np.arange(L))
    ang = pos[:, None] * inv_freq[None, :]
    sin = np.repeat(np.sin(ang), 2, axis=-1)[-T:]
    cos = np.repeat(np.cos(ang), 2, axis=-1)[-T:]
    return sin[:, None, None, :], cos[:, None, None, :]


def rotate_every_two(u):
    return np.stack((-u[..., 1::2], u[..., ::2]), axis=-1).reshape(u.shape)


def apply_rope(u):
    sin, cos = rope_tables()
    u_rot = u[..., :R]
    u_pass = u[..., R:]
    u_rot = u_rot * cos + rotate_every_two(u_rot) * sin
    return np.concatenate([u_rot, u_pass], axis=-1)


def setup_inputs():
    s = kspread(M)
    x = np.random.standard_normal((T, B, M)) * s
    x_words, x_scales = pack4(np.ascontiguousarray(x.reshape(T * B, M).T))
    w = np.random.standard_normal((3 * M, M)) / np.sqrt(M) / s[None, :]
    words, scales = pack4(np.ascontiguousarray(w.T))
    bias = bf(np.random.standard_normal(3 * M) * 0.3)
    return {"x_words": x_words,
            "x_scales": x_scales,
            "in_proj_weight_words": words,
            "in_proj_weight_scales": scales,
            "in_proj_bias": bias}


def reference(x_words, x_scales, in_proj_weight_words, in_proj_weight_scales, in_proj_bias):
    all_out = (unpack4(x_words, x_scales).T.reshape(T, B, M) @ unpack4(in_proj_weight_words, in_proj_weight_scales)) + f64(in_proj_bias)
    q, k, v = np.split(all_out, 3, axis=-1)
    qh = q.reshape(T, B, H, DH)
    kh = k.reshape(T, B, H, DH)
    vh = v.reshape(T, B, H, DH)
    return apply_rope(qh), apply_rope(kh), vh

@@ -1,0 +1,227 @@
+from contextlib import ExitStack
+
+import concourse.mybir as mybir
+from concourse.masks import make_identity
+
+F32 = mybir.dt.float32
+BF16 = mybir.dt.bfloat16
+I32 = mybir.dt.int32
+U8 = mybir.dt.uint8
+FP4X4 = mybir.dt.float4_e2m1fn_x4
+ALU = mybir.AluOpType
+ACT = mybir.ActivationFunctionType
+
+P = 128
+HEAD = 224
+ROT = 112
+PAIRS = ROT // 2
+WIDTH = 3584
+PASSES = WIDTH // 512
+N_OUT = 3 * WIDTH
+CHUNK = 1792
+HEADS_IN_CHUNK = CHUNK // HEAD
+N_CHUNKS = N_OUT // CHUNK
+ROPE_CHUNKS = 2 * WIDTH // CHUNK
+BANKS = ((0, 512), (512, 512), (1024, 512), (1536, 256))
+DEPTH = 4
+PLANE_DEPTH = 3
+
+PI = 3.141592653589793
+TWO_PI = 2.0 * PI
+TWO_PI_HIGH = 6.28125
+TWO_PI_LOW = TWO_PI - TWO_PI_HIGH
+
+FLOPS = 2 * P * WIDTH * N_OUT
+
+
+def tile_multiheadattention_pa_kernel(
+    tc, x_words, x_scales, w_words, w_scales, bias, out_0, out_1, out_2
+):
+    nc = tc.nc
+    outs = [o.rearrange("t b h d -> (t b) (h d)") for o in (out_0, out_1, out_2)]
+
+    with ExitStack() as ctx:
+        keep = ctx.enter_context(tc.tile_pool(name="keep", bufs=1))
+        stage_pool = ctx.enter_context(tc.tile_pool(name="stage", bufs=3))
+        tmp_pool = ctx.enter_context(tc.tile_pool(name="tmp", bufs=2))
+        bias_pool = ctx.enter_context(tc.tile_pool(name="biasp", bufs=2))
+        psum = ctx.enter_context(tc.psum_pool(name="psum", bufs=7))
+        ctx.enter_context(tc.manual_schedule())
+
+        xc = keep.tile([P, PASSES, 256], U8, name="xc", align_bytes=64)
+        xs = keep.tile([P, PASSES, P], U8, name="xs", align_bytes=64)
+        wc = [keep.tile([P, PASSES, 2 * CHUNK], U8, name="wc%d" % i, align_bytes=64) for i in range(DEPTH)]
+        ws = [keep.tile([P, PASSES, CHUNK], U8, name="ws%d" % i, align_bytes=64) for i in range(PLANE_DEPTH)]
+
+        def zero_plane(plane):
+            nc.vector.memset(plane[:].rearrange("p g n -> p (g n)").bitcast(I32), 0)
+
+        def load_scales(c, queue, view):
+            for r in range(4):
+                queue.dma_start(
+                    out=ws[c % PLANE_DEPTH][r:P:32, :, :].bitcast(view),
+                    in_=w_scales[:, r:16:4, c * CHUNK : (c + 1) * CHUNK].rearrange("g q n -> q g n").bitcast(view),
+                )
+
+        def load_codes(c, g0, g1, n0, n):
+            lo = 2 * (c * CHUNK + n0)
+            nc.sync.dma_start(
+                out=wc[c % DEPTH][:, g0:g1, 2 * n0 : 2 * (n0 + n)].bitcast(I32),
+                in_=w_words[g0:g1, :, lo : lo + 2 * n].rearrange("g p n -> p g n").bitcast(I32),
+            )
+
+        def load_chunk(c):
+            load_codes(c, 0, 4, 0, CHUNK)
+            if c < N_CHUNKS - 1:
+                load_codes(c, 4, PASSES, 0, CHUNK)
+            else:
+                load_codes(c, 4, PASSES - 1, 0, CHUNK)
+                for n0, n in BANKS:
+                    load_codes(c, PASSES - 1, PASSES, n0, n)
+
+        zero_plane(xs)
+        zero_plane(ws[0])
+        zb = keep.tile([P, CHUNK], BF16, name="zb")
+        nc.vector.memset(zb[:].bitcast(I32), 0)
+        nc.scalar.dma_start(out=zb[0:N_CHUNKS, :], in_=bias.rearrange("(c n) -> c n", n=CHUNK))
+        zero_plane(ws[1])
+        zero_plane(ws[2])
+        pidx = keep.tile([P, 1], I32, name="pidx")
+        nc.gpsimd.iota(pidx[:], pattern=[[0, 1]], base=0, channel_multiplier=1)
+        ident = keep.tile([P, P], BF16, name="ident")
+        make_identity(nc, ident[:])
+
+        nc.sync.dma_start(out=xc[:].bitcast(I32), in_=x_words.rearrange("g p n -> p g n").bitcast(I32))
+        load_codes(0, 0, 2, 0, CHUNK)
+        for r in range(4):
+            nc.sync.dma_start(
+                out=xs[r:P:32, :, :].bitcast(I32),
+                in_=x_scales[:, r:16:4, :].rearrange("g q n -> q g n").bitcast(I32),
+            )
+        load_scales(0, nc.sync, I32)
+        load_codes(0, 2, 4, 0, CHUNK)
+        load_codes(0, 4, PASSES, 0, CHUNK)
+        load_scales(1, nc.gpsimd, F32)
+        load_scales(2, nc.gpsimd, F32)
+        load_chunk(1)
+
+        tint = keep.tile([P, 1], I32, name="tint")
+        nc.vector.tensor_single_scalar(out=tint[:], in_=pidx[:], scalar=1, op=ALU.arith_shift_right)
+        tcen = keep.tile([P, 1], F32, name="tcen")
+        nc.vector.tensor_scalar(out=tcen[:], in0=tint[:], scalar1=-32.0, scalar2=None, op0=ALU.add)
+        theta = keep.tile([P, PAIRS], F32, name="theta")
+        for i in range(PAIRS):
+            freq = 1.0 / (10000.0 ** (2.0 * i / ROT))
+            mid = 480.0 * freq
+            mid = mid - TWO_PI * round(mid / TWO_PI)
+            nc.vector.tensor_scalar(
+                out=theta[:, i : i + 1], in0=tcen[:], scalar1=freq, scalar2=mid, op0=ALU.mult, op1=ALU.add
+            )
+        arg = keep.tile([P, 2, PAIRS, 2], F32, name="arg")
+        for e in range(2):
+            nc.vector.tensor_scalar(out=arg[:, 0, :, e], in0=theta[:], scalar1=0.5 * PI, scalar2=None, op0=ALU.add)
+        nc.vector.tensor_scalar(out=arg[:, 1, :, 0], in0=theta[:], scalar1=-1.0, scalar2=None, op0=ALU.mult)
+        nc.vector.tensor_copy(out=arg[:, 1, :, 1], in_=theta[:])
+        argf = arg[:].rearrange("p a i e -> p (a i e)")
+        turns = keep.tile([P, 2 * ROT], I32, name="turns")
+        nc.vector.tensor_scalar(out=turns[:], in0=argf, scalar1=1.0 / TWO_PI, scalar2=None, op0=ALU.mult)
+        red1 = keep.tile([P, 2 * ROT], F32, name="red1")
+        nc.vector.scalar_tensor_tensor(
+            out=red1[:], in0=turns[:], scalar=-TWO_PI_HIGH, in1=argf, op0=ALU.mult, op1=ALU.add
+        )
+        red2 = keep.tile([P, 2 * ROT], F32, name="red2")
+        nc.vector.scalar_tensor_tensor(
+            out=red2[:], in0=turns[:], scalar=-TWO_PI_LOW, in1=red1[:], op0=ALU.mult, op1=ALU.add
+        )
+        fix1 = keep.tile([P, 2 * ROT], F32, name="fix1")
+        nc.vector.tensor_scalar(out=fix1[:], in0=red2[:], scalar1=PI, scalar2=-TWO_PI, op0=ALU.is_gt, op1=ALU.mult)
+        red3 = keep.tile([P, 2 * ROT], F32, name="red3")
+        nc.vector.tensor_tensor(out=red3[:], in0=red2[:], in1=fix1[:], op=ALU.add)
+        fix2 = keep.tile([P, 2 * ROT], F32, name="fix2")
+        nc.vector.tensor_scalar(out=fix2[:], in0=red3[:], scalar1=-PI, scalar2=TWO_PI, op0=ALU.is_lt, op1=ALU.mult)
+        red4 = keep.tile([P, 2 * ROT], F32, name="red4")
+        nc.vector.tensor_tensor(out=red4[:], in0=red3[:], in1=fix2[:], op=ALU.add)
+
+        load_chunk(2)
+        load_chunk(3)
+
+        table = keep.tile([P, 2 * ROT], F32, name="table")
+        cos_b = table[:, 0:ROT].unsqueeze(1).to_broadcast([P, HEADS_IN_CHUNK, ROT])
+        sin_b = (
+            table[:, ROT : 2 * ROT]
+            .rearrange("p (i e) -> p i e", e=2)
+            .unsqueeze(1)
+            .to_broadcast([P, HEADS_IN_CHUNK, PAIRS, 2])
+        )
+
+        def mx_pass(c, g, j, acc):
+            n0, n = BANKS[j]
+            nc.tensor.matmul_mx(
+                out=acc[j][:, 0:n],
+                lhsT=xc[:, g, :].bitcast(FP4X4),
+                lhsT_scale=xs[:, g, :],
+                rhs=wc[c % DEPTH][:, g, 2 * n0 : 2 * (n0 + n)].bitcast(FP4X4),
+                rhs_scale=ws[c % PLANE_DEPTH][:, g, n0 : n0 + n],
+                start=(g == 0),
+                stop=(g == PASSES - 1),
+            )
+
+        def spread_bias(c, j, bb):
+            n0, n = BANKS[j]
+            pb = psum.tile([P, 512], F32, name="pb", tag="pb", bufs=1)
+            nc.tensor.matmul(
+                out=pb[:, 0:n],
+                lhsT=ident[:, c : c + 1].to_broadcast([P, P]),
+                rhs=zb[:, n0 : n0 + n],
+                start=True,
+                stop=True,
+            )
+            nc.scalar.copy(out=bb[:, n0 : n0 + n], in_=pb[:, 0:n])
+
+        def add_bias(j, acc, bb, st):
+            n0, n = BANKS[j]
+            nc.vector.tensor_tensor(out=st[:, n0 : n0 + n], in0=acc[j][:, 0:n], in1=bb[:, n0 : n0 + n], op=ALU.add)
+
+        def rope(st):
+            rot = st[:].rearrange("p (h d) -> p h d", d=HEAD)[:, :, 0:ROT]
+            swapped = rot.rearrange("p h (i e) -> p h i e", e=2)[:, :, :, ::-1]
+            t1 = tmp_pool.tile([P, HEADS_IN_CHUNK, ROT], F32, name="t1")
+            t2 = tmp_pool.tile([P, HEADS_IN_CHUNK, ROT], F32, name="t2")
+            nc.vector.tensor_tensor(out=t1[:], in0=rot, in1=cos_b, op=ALU.mult)
+            nc.vector.tensor_tensor(
+                out=t2[:].rearrange("p h (i e) -> p h i e", e=2), in0=swapped, in1=sin_b, op=ALU.mult
+            )
+            nc.vector.tensor_tensor(out=rot, in0=t1[:], in1=t2[:], op=ALU.add)
+
+        waiting = []
+        for c in range(N_CHUNKS):
+            last = c == N_CHUNKS - 1
+            acc = [psum.tile([P, 512], F32, name="acc%d" % j, tag="acc") for j in range(len(BANKS))]
+            bb = bias_pool.tile([P, CHUNK], BF16, name="bb")
+            st = stage_pool.tile([P, CHUNK], F32, name="st")
+            dst = outs[c // 2][:, (c % 2) * CHUNK : (c % 2 + 1) * CHUNK]
+            for g in range(PASSES - 1 if last else PASSES):
+                for j in range(len(BANKS)):
+                    mx_pass(c, g, j, acc)
+                if 1 <= g <= len(BANKS):
+                    spread_bias(c, g - 1, bb)
+            if c == 0:
+                nc.scalar.activation(out=table[:], in_=red4[:], func=ACT.Sin)
+            for old_dst, old_st in waiting:
+                nc.scalar.dma_start(out=old_dst, in_=old_st[:])
+            waiting.clear()
+            if c + PLANE_DEPTH < N_CHUNKS:
+                load_scales(c + PLANE_DEPTH, nc.gpsimd, F32)
+            if c + DEPTH < N_CHUNKS:
+                load_chunk(c + DEPTH)
+            if last:
+                for j, (n0, n) in enumerate(BANKS):
+                    mx_pass(c, PASSES - 1, j, acc)
+                    add_bias(j, acc, bb, st)
+                    nc.scalar.dma_start(out=dst[:, n0 : n0 + n], in_=st[:, n0 : n0 + n])
+            else:
+                for j in range(len(BANKS)):
+                    add_bias(j, acc, bb, st)
+                if c < ROPE_CHUNKS:
+                    rope(st)
+                waiting.append((dst, st))

@@ -57,10 +57,11 @@ def tile_multiheadattention_pa_kernel(
             nc.vector.memset(plane[:].rearrange("p g n -> p (g n)").bitcast(I32), 0)
 
         def load_scales(c, queue, view):
-            for r in range(4):
+            for q in range(8):
+                row = 32 * (q // 4) + q % 4
                 queue.dma_start(
-                    out=ws[c % PLANE_DEPTH][r:P:32, :, :].bitcast(view),
-                    in_=w_scales[:, r:16:4, c * CHUNK : (c + 1) * CHUNK].rearrange("g q n -> q g n").bitcast(view),
+                    out=ws[c % PLANE_DEPTH][row:P:64, :, :].bitcast(view),
+                    in_=w_scales[:, q:16:8, c * CHUNK : (c + 1) * CHUNK].rearrange("g q n -> q g n").bitcast(view),
                 )
 
         def load_codes(c, g0, g1, n0, n):

@@ -44,8 +44,7 @@ def tile_multiheadattention_pa_kernel(
         keep = ctx.enter_context(tc.tile_pool(name="keep", bufs=1))
         stage_pool = ctx.enter_context(tc.tile_pool(name="stage", bufs=3))
         tmp_pool = ctx.enter_context(tc.tile_pool(name="tmp", bufs=2))
-        bias_pool = ctx.enter_context(tc.tile_pool(name="biasp", bufs=2))
-        psum = ctx.enter_context(tc.psum_pool(name="psum", bufs=7))
+        psum = ctx.enter_context(tc.psum_pool(name="psum", bufs=8))
         ctx.enter_context(tc.manual_schedule())
 
         xc = keep.tile([P, PASSES, 256], U8, name="xc", align_bytes=64)
@@ -167,9 +166,11 @@ def tile_multiheadattention_pa_kernel(
                 stop=(g == PASSES - 1),
             )
 
-        def spread_bias(c, j, bb):
+        bb = keep.tile([P, N_CHUNKS, CHUNK], BF16, name="bb")
+
+        def spread_bias(c, j):
             n0, n = BANKS[j]
-            pb = psum.tile([P, 512], F32, name="pb", tag="pb", bufs=1)
+            pb = psum.tile([P, 512], F32, name="pb", tag="acc")
             nc.tensor.matmul(
                 out=pb[:, 0:n],
                 lhsT=ident[:, c : c + 1].to_broadcast([P, P]),
@@ -177,11 +178,11 @@ def tile_multiheadattention_pa_kernel(
                 start=True,
                 stop=True,
             )
-            nc.scalar.copy(out=bb[:, n0 : n0 + n], in_=pb[:, 0:n])
+            nc.scalar.copy(out=bb[:, c, n0 : n0 + n], in_=pb[:, 0:n])
 
-        def add_bias(j, acc, bb, st):
+        def add_bias(c, j, acc, st):
             n0, n = BANKS[j]
-            nc.vector.tensor_tensor(out=st[:, n0 : n0 + n], in0=acc[j][:, 0:n], in1=bb[:, n0 : n0 + n], op=ALU.add)
+            nc.vector.tensor_tensor(out=st[:, n0 : n0 + n], in0=acc[j][:, 0:n], in1=bb[:, c, n0 : n0 + n], op=ALU.add)
 
         def rope(st):
             rot = st[:].rearrange("p (h d) -> p h d", d=HEAD)[:, :, 0:ROT]
@@ -194,23 +195,20 @@ def tile_multiheadattention_pa_kernel(
             )
             nc.vector.tensor_tensor(out=rot, in0=t1[:], in1=t2[:], op=ALU.add)
 
-        waiting = []
+        for c in range(N_CHUNKS):
+            for j in range(len(BANKS)):
+                spread_bias(c, j)
+
         for c in range(N_CHUNKS):
             last = c == N_CHUNKS - 1
             acc = [psum.tile([P, 512], F32, name="acc%d" % j, tag="acc") for j in range(len(BANKS))]
-            bb = bias_pool.tile([P, CHUNK], BF16, name="bb")
             st = stage_pool.tile([P, CHUNK], F32, name="st")
             dst = outs[c // 2][:, (c % 2) * CHUNK : (c % 2 + 1) * CHUNK]
             for g in range(PASSES - 1 if last else PASSES):
                 for j in range(len(BANKS)):
                     mx_pass(c, g, j, acc)
-                if 1 <= g <= len(BANKS):
-                    spread_bias(c, g - 1, bb)
             if c == 0:
                 nc.scalar.activation(out=table[:], in_=red4[:], func=ACT.Sin)
-            for old_dst, old_st in waiting:
-                nc.scalar.dma_start(out=old_dst, in_=old_st[:])
-            waiting.clear()
             if c + PLANE_DEPTH < N_CHUNKS:
                 load_scales(c + PLANE_DEPTH, nc.gpsimd, F32)
             if c + DEPTH < N_CHUNKS:
@@ -218,11 +216,11 @@ def tile_multiheadattention_pa_kernel(
             if last:
                 for j, (n0, n) in enumerate(BANKS):
                     mx_pass(c, PASSES - 1, j, acc)
-                    add_bias(j, acc, bb, st)
+                    add_bias(c, j, acc, st)
                     nc.scalar.dma_start(out=dst[:, n0 : n0 + n], in_=st[:, n0 : n0 + n])
             else:
                 for j in range(len(BANKS)):
-                    add_bias(j, acc, bb, st)
+                    add_bias(c, j, acc, st)
                 if c < ROPE_CHUNKS:
                     rope(st)
-                waiting.append((dst, st))
+                nc.scalar.dma_start(out=dst, in_=st[:])

@@ -71,11 +71,10 @@ def tile_multiheadattention_pa_kernel(
             )
 
         def load_chunk(c):
-            load_codes(c, 0, 4, 0, CHUNK)
             if c < N_CHUNKS - 1:
-                load_codes(c, 4, PASSES, 0, CHUNK)
+                load_codes(c, 0, PASSES, 0, CHUNK)
             else:
-                load_codes(c, 4, PASSES - 1, 0, CHUNK)
+                load_codes(c, 0, PASSES - 1, 0, CHUNK)
                 for n0, n in BANKS:
                     load_codes(c, PASSES - 1, PASSES, n0, n)
 
@@ -99,8 +98,7 @@ def tile_multiheadattention_pa_kernel(
                 in_=x_scales[:, r:16:4, :].rearrange("g q n -> q g n").bitcast(I32),
             )
         load_scales(0, nc.sync, I32)
-        load_codes(0, 2, 4, 0, CHUNK)
-        load_codes(0, 4, PASSES, 0, CHUNK)
+        load_codes(0, 2, PASSES, 0, CHUNK)
         load_scales(1, nc.gpsimd, F32)
         load_scales(2, nc.gpsimd, F32)
         load_chunk(1)

@@ -42,7 +42,7 @@ def tile_multiheadattention_pa_kernel(
 
     with ExitStack() as ctx:
         keep = ctx.enter_context(tc.tile_pool(name="keep", bufs=1))
-        stage_pool = ctx.enter_context(tc.tile_pool(name="stage", bufs=3))
+        stage_pool = ctx.enter_context(tc.tile_pool(name="stage", bufs=N_CHUNKS))
         tmp_pool = ctx.enter_context(tc.tile_pool(name="tmp", bufs=2))
         psum = ctx.enter_context(tc.psum_pool(name="psum", bufs=8))
         ctx.enter_context(tc.manual_schedule())
@@ -215,10 +215,10 @@ def tile_multiheadattention_pa_kernel(
                 for j, (n0, n) in enumerate(BANKS):
                     mx_pass(c, PASSES - 1, j, acc)
                     add_bias(c, j, acc, st)
-                    nc.scalar.dma_start(out=dst[:, n0 : n0 + n], in_=st[:, n0 : n0 + n])
+                    nc.sync.dma_start(out=dst[:, n0 : n0 + n], in_=st[:, n0 : n0 + n])
             else:
                 for j in range(len(BANKS)):
                     add_bias(c, j, acc, st)
                 if c < ROPE_CHUNKS:
                     rope(st)
-                nc.scalar.dma_start(out=dst, in_=st[:])
+                nc.sync.dma_start(out=dst, in_=st[:])

@@ -166,16 +166,17 @@ def tile_multiheadattention_pa_kernel(
 
         bb = keep.tile([P, N_CHUNKS, CHUNK], BF16, name="bb")
 
-        def spread_bias(c, j):
-            n0, n = BANKS[j]
-            pb = psum.tile([P, 512], F32, name="pb", tag="acc")
-            nc.tensor.matmul(
-                out=pb[:, 0:n],
-                lhsT=ident[:, c : c + 1].to_broadcast([P, P]),
-                rhs=zb[:, n0 : n0 + n],
-                start=True,
-                stop=True,
-            )
+        def spread_bias(c, n0, n):
+            pb = psum.tile([P, 1024], BF16, name="pb", tag="acc")
+            for m0 in range(0, n, 512):
+                m = min(512, n - m0)
+                nc.tensor.matmul(
+                    out=pb[:, m0 : m0 + m],
+                    lhsT=ident[:, c : c + 1].to_broadcast([P, P]),
+                    rhs=zb[:, n0 + m0 : n0 + m0 + m],
+                    start=True,
+                    stop=True,
+                )
             nc.scalar.copy(out=bb[:, c, n0 : n0 + n], in_=pb[:, 0:n])
 
         def add_bias(c, j, acc, st):
@@ -194,8 +195,8 @@ def tile_multiheadattention_pa_kernel(
             nc.vector.tensor_tensor(out=rot, in0=t1[:], in1=t2[:], op=ALU.add)
 
         for c in range(N_CHUNKS):
-            for j in range(len(BANKS)):
-                spread_bias(c, j)
+            spread_bias(c, 0, 1024)
+            spread_bias(c, 1024, CHUNK - 1024)
 
         for c in range(N_CHUNKS):
             last = c == N_CHUNKS - 1

@@ -47,10 +47,10 @@ def tile_multiheadattention_pa_kernel(
         psum = ctx.enter_context(tc.psum_pool(name="psum", bufs=8))
         ctx.enter_context(tc.manual_schedule())
 
-        xc = keep.tile([P, PASSES, 256], U8, name="xc", align_bytes=64)
-        xs = keep.tile([P, PASSES, P], U8, name="xs", align_bytes=64)
-        wc = [keep.tile([P, PASSES, 2 * CHUNK], U8, name="wc%d" % i, align_bytes=64) for i in range(DEPTH)]
-        ws = [keep.tile([P, PASSES, CHUNK], U8, name="ws%d" % i, align_bytes=64) for i in range(PLANE_DEPTH)]
+        xc = keep.tile([P, PASSES, 256], U8, name="xc", align_bytes=256)
+        xs = keep.tile([P, PASSES, P], U8, name="xs", align_bytes=256)
+        wc = [keep.tile([P, PASSES, 2 * CHUNK], U8, name="wc%d" % i, align_bytes=256) for i in range(DEPTH)]
+        ws = [keep.tile([P, PASSES, CHUNK], U8, name="ws%d" % i, align_bytes=256) for i in range(PLANE_DEPTH)]
 
         def zero_plane(plane):
             nc.vector.memset(plane[:].rearrange("p g n -> p (g n)").bitcast(I32), 0)
@@ -201,7 +201,7 @@ def tile_multiheadattention_pa_kernel(
         for c in range(N_CHUNKS):
             last = c == N_CHUNKS - 1
             acc = [psum.tile([P, 512], F32, name="acc%d" % j, tag="acc") for j in range(len(BANKS))]
-            st = stage_pool.tile([P, CHUNK], F32, name="st")
+            st = stage_pool.tile([P, CHUNK], F32, name="st", align_bytes=256)
             dst = outs[c // 2][:, (c % 2) * CHUNK : (c % 2 + 1) * CHUNK]
             for g in range(PASSES - 1 if last else PASSES):
                 for j in range(len(BANKS)):

@@ -23,6 +23,8 @@ HEADS_IN_CHUNK = CHUNK // HEAD
 N_CHUNKS = N_OUT // CHUNK
 ROPE_CHUNKS = 2 * WIDTH // CHUNK
 BANKS = ((0, 512), (512, 512), (1024, 512), (1536, 256))
+LAST_PIECES = ((0, 1024), (1024, 768))
+SPLIT_FROM = 3
 DEPTH = 4
 PLANE_DEPTH = 3
 
@@ -71,12 +73,18 @@ def tile_multiheadattention_pa_kernel(
             )
 
         def load_chunk(c):
-            if c < N_CHUNKS - 1:
+            if c < SPLIT_FROM:
                 load_codes(c, 0, PASSES, 0, CHUNK)
+            elif c < N_CHUNKS - 1:
+                load_codes(c, 0, 4, 0, CHUNK)
+                load_codes(c, 4, PASSES, 0, CHUNK)
             else:
-                load_codes(c, 0, PASSES - 1, 0, CHUNK)
-                for n0, n in BANKS:
-                    load_codes(c, PASSES - 1, PASSES, n0, n)
+                load_codes(c, 0, 3, 0, CHUNK)
+                load_codes(c, 3, PASSES - 1, 0, CHUNK)
+
+        def load_last_pass():
+            for n0, n in LAST_PIECES:
+                load_codes(N_CHUNKS - 1, PASSES - 1, PASSES, n0, n)
 
         zero_plane(xs)
         zero_plane(ws[0])
@@ -212,6 +220,8 @@ def tile_multiheadattention_pa_kernel(
                 load_scales(c + PLANE_DEPTH, nc.gpsimd, F32)
             if c + DEPTH < N_CHUNKS:
                 load_chunk(c + DEPTH)
+            if c == 3:
+                load_last_pass()
             if last:
                 for j, (n0, n) in enumerate(BANKS):
                     mx_pass(c, PASSES - 1, j, acc)
@@ -222,4 +232,4 @@ def tile_multiheadattention_pa_kernel(
                     add_bias(c, j, acc, st)
                 if c < ROPE_CHUNKS:
                     rope(st)
-                nc.sync.dma_start(out=dst, in_=st[:])
+                nc.scalar.dma_start(out=dst, in_=st[:])

@@ -58,7 +58,7 @@ def tile_multiheadattention_pa_kernel(
             nc.vector.memset(plane[:].rearrange("p g n -> p (g n)").bitcast(I32), 0)
 
         def load_scales(c, queue, view):
-            for q in range(8):
+            for q in (0, 4, 1, 5, 2, 6, 3, 7):
                 row = 32 * (q // 4) + q % 4
                 queue.dma_start(
                     out=ws[c % PLANE_DEPTH][row:P:64, :, :].bitcast(view),

@@ -25,6 +25,7 @@ ROPE_CHUNKS = 2 * WIDTH // CHUNK
 BANKS = ((0, 512), (512, 512), (1024, 512), (1536, 256))
 LAST_PIECES = ((0, 1024), (1024, 768))
 SPLIT_FROM = 3
+PACE_COLUMNS = 800
 DEPTH = 4
 PLANE_DEPTH = 3
 
@@ -64,6 +65,16 @@ def tile_multiheadattention_pa_kernel(
                     out=ws[c % PLANE_DEPTH][row:P:64, :, :].bitcast(view),
                     in_=w_scales[:, q:16:8, c * CHUNK : (c + 1) * CHUNK].rearrange("g q n -> q g n").bitcast(view),
                 )
+
+        pace = keep.tile([P, PACE_COLUMNS], F32, name="pace")
+
+        def load_scales_paced(c):
+            for r in range(4):
+                nc.gpsimd.dma_start(
+                    out=ws[c % PLANE_DEPTH][r:P:32, :, :].bitcast(F32),
+                    in_=w_scales[:, r:16:4, c * CHUNK : (c + 1) * CHUNK].rearrange("g q n -> q g n").bitcast(F32),
+                )
+                nc.gpsimd.memset(pace[:], 0.0)
 
         def load_codes(c, g0, g1, n0, n):
             lo = 2 * (c * CHUNK + n0)
@@ -107,8 +118,8 @@ def tile_multiheadattention_pa_kernel(
             )
         load_scales(0, nc.sync, I32)
         load_codes(0, 2, PASSES, 0, CHUNK)
-        load_scales(1, nc.gpsimd, F32)
-        load_scales(2, nc.gpsimd, F32)
+        load_scales_paced(1)
+        load_scales_paced(2)
         load_chunk(1)
 
         tint = keep.tile([P, 1], I32, name="tint")
@@ -217,7 +228,7 @@ def tile_multiheadattention_pa_kernel(
             if c == 0:
                 nc.scalar.activation(out=table[:], in_=red4[:], func=ACT.Sin)
             if c + PLANE_DEPTH < N_CHUNKS:
-                load_scales(c + PLANE_DEPTH, nc.gpsimd, F32)
+                load_scales_paced(c + PLANE_DEPTH)
             if c + DEPTH < N_CHUNKS:
                 load_chunk(c + DEPTH)
             if c == 3:

@@ -25,7 +25,7 @@ ROPE_CHUNKS = 2 * WIDTH // CHUNK
 BANKS = ((0, 512), (512, 512), (1024, 512), (1536, 256))
 LAST_PIECES = ((0, 1024), (1024, 768))
 SPLIT_FROM = 3
-PACE_COLUMNS = 800
+PACE_COLUMNS = 1600
 DEPTH = 4
 PLANE_DEPTH = 3
 

@@ -25,6 +25,7 @@ ROPE_CHUNKS = 2 * WIDTH // CHUNK
 BANKS = ((0, 512), (512, 512), (1024, 512), (1536, 256))
 LAST_PIECES = ((0, 1024), (1024, 768))
 SPLIT_FROM = 3
+EARLY_STORES = 3
 PACE_COLUMNS = 1600
 DEPTH = 4
 PLANE_DEPTH = 3
@@ -243,4 +244,4 @@ def tile_multiheadattention_pa_kernel(
                     add_bias(c, j, acc, st)
                 if c < ROPE_CHUNKS:
                     rope(st)
-                nc.scalar.dma_start(out=dst, in_=st[:])
+                (nc.scalar if c < EARLY_STORES else nc.sync).dma_start(out=dst, in_=st[:])

@@ -26,7 +26,7 @@ BANKS = ((0, 512), (512, 512), (1024, 512), (1536, 256))
 LAST_PIECES = ((0, 1024), (1024, 768))
 SPLIT_FROM = 3
 EARLY_STORES = 3
-PACE_COLUMNS = 1600
+PACE_COLUMNS = 800
 DEPTH = 4
 PLANE_DEPTH = 3
 
@@ -68,6 +68,7 @@ def tile_multiheadattention_pa_kernel(
                 )
 
         pace = keep.tile([P, PACE_COLUMNS], F32, name="pace")
+        gate = keep.tile([P, 1], F32, name="gate")
 
         def load_scales_paced(c):
             for r in range(4):
@@ -228,8 +229,6 @@ def tile_multiheadattention_pa_kernel(
                     mx_pass(c, g, j, acc)
             if c == 0:
                 nc.scalar.activation(out=table[:], in_=red4[:], func=ACT.Sin)
-            if c + PLANE_DEPTH < N_CHUNKS:
-                load_scales_paced(c + PLANE_DEPTH)
             if c + DEPTH < N_CHUNKS:
                 load_chunk(c + DEPTH)
             if c == 3:
@@ -242,6 +241,9 @@ def tile_multiheadattention_pa_kernel(
             else:
                 for j in range(len(BANKS)):
                     add_bias(c, j, acc, st)
+                if c + PLANE_DEPTH < N_CHUNKS:
+                    nc.gpsimd.tensor_copy(out=gate[:], in_=st[:, CHUNK - 1 : CHUNK])
+                    load_scales_paced(c + PLANE_DEPTH)
                 if c < ROPE_CHUNKS:
                     rope(st)
                 (nc.scalar if c < EARLY_STORES else nc.sync).dma_start(out=dst, in_=st[:])

@@ -26,7 +26,7 @@ BANKS = ((0, 512), (512, 512), (1024, 512), (1536, 256))
 LAST_PIECES = ((0, 1024), (1024, 768))
 SPLIT_FROM = 3
 EARLY_STORES = 3
-PACE_COLUMNS = 800
+SCALE_SLICES = ((0, 4), (4, 7))
 DEPTH = 4
 PLANE_DEPTH = 3
 
@@ -67,16 +67,17 @@ def tile_multiheadattention_pa_kernel(
                     in_=w_scales[:, q:16:8, c * CHUNK : (c + 1) * CHUNK].rearrange("g q n -> q g n").bitcast(view),
                 )
 
-        pace = keep.tile([P, PACE_COLUMNS], F32, name="pace")
         gate = keep.tile([P, 1], F32, name="gate")
 
         def load_scales_paced(c):
-            for r in range(4):
-                nc.gpsimd.dma_start(
-                    out=ws[c % PLANE_DEPTH][r:P:32, :, :].bitcast(F32),
-                    in_=w_scales[:, r:16:4, c * CHUNK : (c + 1) * CHUNK].rearrange("g q n -> q g n").bitcast(F32),
-                )
-                nc.gpsimd.memset(pace[:], 0.0)
+            for g0, g1 in SCALE_SLICES:
+                for r in range(4):
+                    nc.gpsimd.dma_start(
+                        out=ws[c % PLANE_DEPTH][r:P:32, g0:g1, :].bitcast(F32),
+                        in_=w_scales[g0:g1, r:16:4, c * CHUNK : (c + 1) * CHUNK]
+                        .rearrange("g q n -> q g n")
+                        .bitcast(F32),
+                    )
 
         def load_codes(c, g0, g1, n0, n):
             lo = 2 * (c * CHUNK + n0)

from contextlib import ExitStack

import concourse.mybir as mybir
from concourse.masks import make_identity

F32 = mybir.dt.float32
BF16 = mybir.dt.bfloat16
I32 = mybir.dt.int32
U8 = mybir.dt.uint8
FP4X4 = mybir.dt.float4_e2m1fn_x4
ALU = mybir.AluOpType
ACT = mybir.ActivationFunctionType

P = 128
HEAD = 224
ROT = 112
PAIRS = ROT // 2
WIDTH = 3584
PASSES = WIDTH // 512
N_OUT = 3 * WIDTH
CHUNK = 1792
HEADS_IN_CHUNK = CHUNK // HEAD
N_CHUNKS = N_OUT // CHUNK
ROPE_CHUNKS = 2 * WIDTH // CHUNK
BANKS = ((0, 512), (512, 512), (1024, 512), (1536, 256))
LAST_PIECES = ((0, 1024), (1024, 768))
SPLIT_FROM = 3
EARLY_STORES = 3
SCALE_SLICES = ((0, 4), (4, 7))
DEPTH = 4
PLANE_DEPTH = 3

PI = 3.141592653589793
TWO_PI = 2.0 * PI
TWO_PI_HIGH = 6.28125
TWO_PI_LOW = TWO_PI - TWO_PI_HIGH

FLOPS = 2 * P * WIDTH * N_OUT


def tile_multiheadattention_pa_kernel(
    tc, x_words, x_scales, w_words, w_scales, bias, out_0, out_1, out_2
):
    nc = tc.nc
    outs = [o.rearrange("t b h d -> (t b) (h d)") for o in (out_0, out_1, out_2)]

    with ExitStack() as ctx:
        keep = ctx.enter_context(tc.tile_pool(name="keep", bufs=1))
        stage_pool = ctx.enter_context(tc.tile_pool(name="stage", bufs=N_CHUNKS))
        tmp_pool = ctx.enter_context(tc.tile_pool(name="tmp", bufs=2))
        psum = ctx.enter_context(tc.psum_pool(name="psum", bufs=8))
        ctx.enter_context(tc.manual_schedule())

        xc = keep.tile([P, PASSES, 256], U8, name="xc", align_bytes=256)
        xs = keep.tile([P, PASSES, P], U8, name="xs", align_bytes=256)
        wc = [keep.tile([P, PASSES, 2 * CHUNK], U8, name="wc%d" % i, align_bytes=256) for i in range(DEPTH)]
        ws = [keep.tile([P, PASSES, CHUNK], U8, name="ws%d" % i, align_bytes=256) for i in range(PLANE_DEPTH)]

        def zero_plane(plane):
            nc.vector.memset(plane[:].rearrange("p g n -> p (g n)").bitcast(I32), 0)

        def load_scales(c, queue, view):
            for q in (0, 4, 1, 5, 2, 6, 3, 7):
                row = 32 * (q // 4) + q % 4
                queue.dma_start(
                    out=ws[c % PLANE_DEPTH][row:P:64, :, :].bitcast(view),
                    in_=w_scales[:, q:16:8, c * CHUNK : (c + 1) * CHUNK].rearrange("g q n -> q g n").bitcast(view),
                )

        gate = keep.tile([P, 1], F32, name="gate")

        def load_scales_paced(c):
            for g0, g1 in SCALE_SLICES:
                for r in range(4):
                    nc.gpsimd.dma_start(
                        out=ws[c % PLANE_DEPTH][r:P:32, g0:g1, :].bitcast(F32),
                        in_=w_scales[g0:g1, r:16:4, c * CHUNK : (c + 1) * CHUNK]
                        .rearrange("g q n -> q g n")
                        .bitcast(F32),
                    )

        def load_codes(c, g0, g1, n0, n):
            lo = 2 * (c * CHUNK + n0)
            nc.sync.dma_start(
                out=wc[c % DEPTH][:, g0:g1, 2 * n0 : 2 * (n0 + n)].bitcast(I32),
                in_=w_words[g0:g1, :, lo : lo + 2 * n].rearrange("g p n -> p g n").bitcast(I32),
            )

        def load_chunk(c):
            if c < SPLIT_FROM:
                load_codes(c, 0, PASSES, 0, CHUNK)
            elif c < N_CHUNKS - 1:
                load_codes(c, 0, 4, 0, CHUNK)
                load_codes(c, 4, PASSES, 0, CHUNK)
            else:
                load_codes(c, 0, 3, 0, CHUNK)
                load_codes(c, 3, PASSES - 1, 0, CHUNK)

        def load_last_pass():
            for n0, n in LAST_PIECES:
                load_codes(N_CHUNKS - 1, PASSES - 1, PASSES, n0, n)

        zero_plane(xs)
        zero_plane(ws[0])
        zb = keep.tile([P, CHUNK], BF16, name="zb")
        nc.vector.memset(zb[:].bitcast(I32), 0)
        nc.scalar.dma_start(out=zb[0:N_CHUNKS, :], in_=bias.rearrange("(c n) -> c n", n=CHUNK))
        zero_plane(ws[1])
        zero_plane(ws[2])
        pidx = keep.tile([P, 1], I32, name="pidx")
        nc.gpsimd.iota(pidx[:], pattern=[[0, 1]], base=0, channel_multiplier=1)
        ident = keep.tile([P, P], BF16, name="ident")
        make_identity(nc, ident[:])

        nc.sync.dma_start(out=xc[:].bitcast(I32), in_=x_words.rearrange("g p n -> p g n").bitcast(I32))
        load_codes(0, 0, 2, 0, CHUNK)
        for r in range(4):
            nc.sync.dma_start(
                out=xs[r:P:32, :, :].bitcast(I32),
                in_=x_scales[:, r:16:4, :].rearrange("g q n -> q g n").bitcast(I32),
            )
        load_scales(0, nc.sync, I32)
        load_codes(0, 2, PASSES, 0, CHUNK)
        load_scales_paced(1)
        load_scales_paced(2)
        load_chunk(1)

        tint = keep.tile([P, 1], I32, name="tint")
        nc.vector.tensor_single_scalar(out=tint[:], in_=pidx[:], scalar=1, op=ALU.arith_shift_right)
        tcen = keep.tile([P, 1], F32, name="tcen")
        nc.vector.tensor_scalar(out=tcen[:], in0=tint[:], scalar1=-32.0, scalar2=None, op0=ALU.add)
        theta = keep.tile([P, PAIRS], F32, name="theta")
        for i in range(PAIRS):
            freq = 1.0 / (10000.0 ** (2.0 * i / ROT))
            mid = 480.0 * freq
            mid = mid - TWO_PI * round(mid / TWO_PI)
            nc.vector.tensor_scalar(
                out=theta[:, i : i + 1], in0=tcen[:], scalar1=freq, scalar2=mid, op0=ALU.mult, op1=ALU.add
            )
        arg = keep.tile([P, 2, PAIRS, 2], F32, name="arg")
        for e in range(2):
            nc.vector.tensor_scalar(out=arg[:, 0, :, e], in0=theta[:], scalar1=0.5 * PI, scalar2=None, op0=ALU.add)
        nc.vector.tensor_scalar(out=arg[:, 1, :, 0], in0=theta[:], scalar1=-1.0, scalar2=None, op0=ALU.mult)
        nc.vector.tensor_copy(out=arg[:, 1, :, 1], in_=theta[:])
        argf = arg[:].rearrange("p a i e -> p (a i e)")
        turns = keep.tile([P, 2 * ROT], I32, name="turns")
        nc.vector.tensor_scalar(out=turns[:], in0=argf, scalar1=1.0 / TWO_PI, scalar2=None, op0=ALU.mult)
        red1 = keep.tile([P, 2 * ROT], F32, name="red1")
        nc.vector.scalar_tensor_tensor(
            out=red1[:], in0=turns[:], scalar=-TWO_PI_HIGH, in1=argf, op0=ALU.mult, op1=ALU.add
        )
        red2 = keep.tile([P, 2 * ROT], F32, name="red2")
        nc.vector.scalar_tensor_tensor(
            out=red2[:], in0=turns[:], scalar=-TWO_PI_LOW, in1=red1[:], op0=ALU.mult, op1=ALU.add
        )
        fix1 = keep.tile([P, 2 * ROT], F32, name="fix1")
        nc.vector.tensor_scalar(out=fix1[:], in0=red2[:], scalar1=PI, scalar2=-TWO_PI, op0=ALU.is_gt, op1=ALU.mult)
        red3 = keep.tile([P, 2 * ROT], F32, name="red3")
        nc.vector.tensor_tensor(out=red3[:], in0=red2[:], in1=fix1[:], op=ALU.add)
        fix2 = keep.tile([P, 2 * ROT], F32, name="fix2")
        nc.vector.tensor_scalar(out=fix2[:], in0=red3[:], scalar1=-PI, scalar2=TWO_PI, op0=ALU.is_lt, op1=ALU.mult)
        red4 = keep.tile([P, 2 * ROT], F32, name="red4")
        nc.vector.tensor_tensor(out=red4[:], in0=red3[:], in1=fix2[:], op=ALU.add)

        load_chunk(2)
        load_chunk(3)

        table = keep.tile([P, 2 * ROT], F32, name="table")
        cos_b = table[:, 0:ROT].unsqueeze(1).to_broadcast([P, HEADS_IN_CHUNK, ROT])
        sin_b = (
            table[:, ROT : 2 * ROT]
            .rearrange("p (i e) -> p i e", e=2)
            .unsqueeze(1)
            .to_broadcast([P, HEADS_IN_CHUNK, PAIRS, 2])
        )

        def mx_pass(c, g, j, acc):
            n0, n = BANKS[j]
            nc.tensor.matmul_mx(
                out=acc[j][:, 0:n],
                lhsT=xc[:, g, :].bitcast(FP4X4),
                lhsT_scale=xs[:, g, :],
                rhs=wc[c % DEPTH][:, g, 2 * n0 : 2 * (n0 + n)].bitcast(FP4X4),
                rhs_scale=ws[c % PLANE_DEPTH][:, g, n0 : n0 + n],
                start=(g == 0),
                stop=(g == PASSES - 1),
            )

        bb = keep.tile([P, N_CHUNKS, CHUNK], BF16, name="bb")

        def spread_bias(c, n0, n):
            pb = psum.tile([P, 1024], BF16, name="pb", tag="acc")
            for m0 in range(0, n, 512):
                m = min(512, n - m0)
                nc.tensor.matmul(
                    out=pb[:, m0 : m0 + m],
                    lhsT=ident[:, c : c + 1].to_broadcast([P, P]),
                    rhs=zb[:, n0 + m0 : n0 + m0 + m],
                    start=True,
                    stop=True,
                )
            nc.scalar.copy(out=bb[:, c, n0 : n0 + n], in_=pb[:, 0:n])

        def add_bias(c, j, acc, st):
            n0, n = BANKS[j]
            nc.vector.tensor_tensor(out=st[:, n0 : n0 + n], in0=acc[j][:, 0:n], in1=bb[:, c, n0 : n0 + n], op=ALU.add)

        def rope(st):
            rot = st[:].rearrange("p (h d) -> p h d", d=HEAD)[:, :, 0:ROT]
            swapped = rot.rearrange("p h (i e) -> p h i e", e=2)[:, :, :, ::-1]
            t1 = tmp_pool.tile([P, HEADS_IN_CHUNK, ROT], F32, name="t1")
            t2 = tmp_pool.tile([P, HEADS_IN_CHUNK, ROT], F32, name="t2")
            nc.vector.tensor_tensor(out=t1[:], in0=rot, in1=cos_b, op=ALU.mult)
            nc.vector.tensor_tensor(
                out=t2[:].rearrange("p h (i e) -> p h i e", e=2), in0=swapped, in1=sin_b, op=ALU.mult
            )
            nc.vector.tensor_tensor(out=rot, in0=t1[:], in1=t2[:], op=ALU.add)

        for c in range(N_CHUNKS):
            spread_bias(c, 0, 1024)
            spread_bias(c, 1024, CHUNK - 1024)

        for c in range(N_CHUNKS):
            last = c == N_CHUNKS - 1
            acc = [psum.tile([P, 512], F32, name="acc%d" % j, tag="acc") for j in range(len(BANKS))]
            st = stage_pool.tile([P, CHUNK], F32, name="st", align_bytes=256)
            dst = outs[c // 2][:, (c % 2) * CHUNK : (c % 2 + 1) * CHUNK]
            for g in range(PASSES - 1 if last else PASSES):
                for j in range(len(BANKS)):
                    mx_pass(c, g, j, acc)
            if c == 0:
                nc.scalar.activation(out=table[:], in_=red4[:], func=ACT.Sin)
            if c + DEPTH < N_CHUNKS:
                load_chunk(c + DEPTH)
            if c == 3:
                load_last_pass()
            if last:
                for j, (n0, n) in enumerate(BANKS):
                    mx_pass(c, PASSES - 1, j, acc)
                    add_bias(c, j, acc, st)
                    nc.sync.dma_start(out=dst[:, n0 : n0 + n], in_=st[:, n0 : n0 + n])
            else:
                for j in range(len(BANKS)):
                    add_bias(c, j, acc, st)
                if c + PLANE_DEPTH < N_CHUNKS:
                    nc.gpsimd.tensor_copy(out=gate[:], in_=st[:, CHUNK - 1 : CHUNK])
                    load_scales_paced(c + PLANE_DEPTH)
                if c < ROPE_CHUNKS:
                    rope(st)
                (nc.scalar if c < EARLY_STORES else nc.sync).dma_start(out=dst, in_=st[:])
